import numpy as np
import ml_dtypes


def mxq(x, axis, fmt="e4m3"):
    dtype, down = {"e4m3": (ml_dtypes.float8_e4m3fn, 7), "e5m2": (ml_dtypes.float8_e5m2, 14)}[fmt]
    v = np.moveaxis(np.asarray(x, np.float32).astype(ml_dtypes.bfloat16).astype(np.float64), axis, -1)
    blocks = v.reshape(v.shape[:-1] + (-1, 32))
    amax = np.abs(blocks).max(-1, keepdims=True)
    byte = np.maximum(np.where(amax > 0, np.frexp(amax)[1] - 1 + 127, 0) - down, 1)
    scale = np.exp2(byte - 127.0)
    codes = (blocks / scale).astype(np.float32).astype(dtype).astype(np.float64)
    return np.moveaxis((codes * scale).reshape(v.shape), -1, axis)


WIDE = False


def mx_kscale(k):
    if not WIDE:
        return np.ones(k)
    levels = np.array([10, -10, 5, -5, 0])
    a = np.random.permutation(np.resize(levels, k // 512 * 4)).reshape(k // 512, 4)
    idx = np.arange(k)
    return np.exp2(a[idx // 512, idx % 128 // 32])


BF16 = ml_dtypes.bfloat16


def bf(x):
    return np.asarray(x, np.float32).astype(BF16)


def f64(x):
    return np.asarray(x).astype(np.float64)


B, S, Dm, H = 2, 128, 2048, 16
D = Dm // H
ROPE_BASE = 10000.0


def _rope(t):
    theta = 1.0 / (ROPE_BASE ** (np.arange(0, D, 2, dtype=np.float64) / D))
    pos = np.arange(H, dtype=np.float64)[:, None]
    ang = pos * theta
    sin, cos = np.sin(ang), np.cos(ang)
    te, to = t[..., 0::2], t[..., 1::2]
    re = te * cos - to * sin
    ro = te * sin + to * cos
    return np.stack([re, ro], axis=-1).reshape(B, S, H, D)


def setup_inputs():
    s = mx_kscale(Dm)
    sc = 1.0 / np.sqrt(Dm)
    return {"x": bf(np.random.standard_normal((B, S, Dm)) * s),
            "Wq": bf(np.random.standard_normal((Dm, Dm)) * sc / s[:, None]),
            "Wk": bf(np.random.standard_normal((Dm, Dm)) * sc / s[:, None]),
            "Wv": bf(np.random.standard_normal((Dm, Dm)) * sc / s[:, None]),
            "st_pos": 0}


def reference(x, Wq, Wk, Wv, st_pos):
    xq = mxq(f64(x), 2, "e4m3")
    q = (xq @ mxq(f64(Wq), 0, "e4m3")).reshape(B, S, H, D)
    k = (xq @ mxq(f64(Wk), 0, "e4m3")).reshape(B, S, H, D)
    v = (xq @ mxq(f64(Wv), 0, "e4m3")).reshape(B, S, H, D)
    q = _rope(q)
    k = _rope(k)
    return q, k, v

@@ -1,0 +1,225 @@
+import math
+from contextlib import ExitStack
+
+import concourse.mybir as mybir
+from concourse.masks import make_identity
+
+F32 = mybir.dt.float32
+BF16 = mybir.dt.bfloat16
+U32 = mybir.dt.uint32
+U8 = mybir.dt.uint8
+I32 = mybir.dt.int32
+FP8X4 = mybir.dt.float8_e4m3fn_x4
+ALU = mybir.AluOpType
+ACT = mybir.ActivationFunctionType
+
+P = 128
+N_BATCH = 2
+DM = 2048
+HEADS = 16
+HEAD = 128
+PACK = 4
+K_PASS = P * PACK
+N_PASS = DM // K_PASS
+CHUNK = 512
+N_CHUNK = DM // CHUNK
+TOKENS = N_BATCH * P
+ROPE_BASE = 10000.0
+
+FLOPS = 2 * TOKENS * DM * 3 * DM
+
+V_COLS = (256, 256, 256, 256, 384, 384, 256, 256, 384, 384, 256, 256)
+
+
+def tile_selfattention_kernel(tc, x, Wq, Wk, Wv, st_pos, out_0, out_1, out_2):
+    nc = tc.nc
+    weights = (Wq, Wk, Wv)
+    outs = (out_0, out_1, out_2)
+
+    with ExitStack() as ctx:
+        const = ctx.enter_context(tc.tile_pool(name="const", bufs=1))
+        rawp = ctx.enter_context(tc.tile_pool(name="rawp", bufs=4))
+        grpp = ctx.enter_context(tc.tile_pool(name="grpp", bufs=8))
+        codep = ctx.enter_context(tc.tile_pool(name="codep", bufs=16))
+        tsbp = ctx.enter_context(tc.tile_pool(name="tsbp", bufs=4))
+        outp = ctx.enter_context(tc.tile_pool(name="outp", bufs=4))
+        psum = ctx.enter_context(tc.psum_pool(name="psum", bufs=1))
+
+        def bank(i, shape, label):
+            return psum.tile(shape, F32, name="%s%d" % (label, i), tag="bank%d" % i)
+
+        x_sb = []
+        for b in range(N_BATCH):
+            xb = const.tile([P, DM], BF16, name="x_sb%d" % b)
+            nc.sync.dma_start(out=xb[:], in_=x[b])
+            x_sb.append(xb)
+
+        ident = const.tile([P, P], F32, name="ident")
+        make_identity(nc, ident[:])
+        pidx_i = const.tile([P, 1], I32, name="pidx_i")
+        nc.gpsimd.iota(pidx_i[:], pattern=[[0, 1]], base=0, channel_multiplier=1)
+        hcol_i = const.tile([P, HEADS], I32, name="hcol_i")
+        nc.gpsimd.iota(hcol_i[:], pattern=[[1, HEADS]], base=0, channel_multiplier=0)
+
+        half_i = const.tile([P, 1], I32, name="half_i")
+        nc.vector.tensor_single_scalar(out=half_i[:], in_=pidx_i[:], scalar=1, op=ALU.arith_shift_right)
+        par_i = const.tile([P, 1], I32, name="par_i")
+        nc.vector.tensor_single_scalar(out=par_i[:], in_=pidx_i[:], scalar=1, op=ALU.bitwise_and)
+        half_f = const.tile([P, 1], F32, name="half_f")
+        nc.vector.tensor_copy(out=half_f[:], in_=half_i[:])
+        par_f = const.tile([P, 1], F32, name="par_f")
+        nc.vector.tensor_copy(out=par_f[:], in_=par_i[:])
+        hcol_f = const.tile([P, HEADS], F32, name="hcol_f")
+        nc.vector.tensor_copy(out=hcol_f[:], in_=hcol_i[:])
+        sgn = const.tile([P, 1], F32, name="sgn")
+        nc.vector.tensor_scalar(out=sgn[:], in0=par_f[:], scalar1=-2.0, scalar2=1.0, op0=ALU.mult, op1=ALU.add)
+
+        theta = const.tile([P, 1], F32, name="theta")
+        nc.scalar.activation(out=theta[:], in_=half_f[:], func=ACT.Exp, scale=-math.log(ROPE_BASE) / (HEAD // 2))
+
+        turns = const.tile([P, 2 * HEADS], F32, name="turns")
+        nc.vector.tensor_scalar(
+            out=turns[:, 0:HEADS], in0=hcol_f[:], scalar1=theta[:, 0:1], scalar2=1.0 / (2.0 * math.pi),
+            op0=ALU.mult, op1=ALU.mult,
+        )
+        nc.vector.tensor_scalar(
+            out=turns[:, HEADS : 2 * HEADS], in0=turns[:, 0:HEADS], scalar1=0.25, scalar2=None, op0=ALU.add
+        )
+        red1 = const.tile([P, 2 * HEADS], F32, name="red1")
+        nc.vector.scalar_tensor_tensor(out=red1[:], in0=turns[:], scalar=0.5, in1=turns[:], op0=ALU.is_gt, op1=ALU.subtract)
+        red2 = const.tile([P, 2 * HEADS], F32, name="red2")
+        nc.vector.scalar_tensor_tensor(out=red2[:], in0=turns[:], scalar=1.5, in1=red1[:], op0=ALU.is_gt, op1=ALU.add)
+        red3 = const.tile([P, 2 * HEADS], F32, name="red3")
+        nc.vector.scalar_tensor_tensor(out=red3[:], in0=turns[:], scalar=2.5, in1=red2[:], op0=ALU.is_gt, op1=ALU.add)
+        trig = const.tile([P, 2 * HEADS], F32, name="trig")
+        nc.scalar.activation(out=trig[:], in_=red3[:], func=ACT.Sin, scale=-2.0 * math.pi)
+        sin_p = const.tile([P, HEADS], F32, name="sin_p")
+        nc.vector.tensor_scalar(out=sin_p[:], in0=trig[:, 0:HEADS], scalar1=sgn[:, 0:1], scalar2=None, op0=ALU.mult)
+
+        swap = const.tile([P, P], F32, name="swap")
+        swap_v = swap[:].rearrange("p (i e) -> p i e", e=2)
+        ident_v = ident[:].rearrange("p (i e) -> p i e", e=2)
+        nc.vector.tensor_copy(out=swap_v[:, :, 0], in_=ident_v[:, :, 1])
+        nc.vector.tensor_copy(out=swap_v[:, :, 1], in_=ident_v[:, :, 0])
+
+        gx = const.tile([P, TOKENS * N_PASS * PACK], BF16, name="gx", align_bytes=64)
+        gx_v = gx[:].bitcast(F32).rearrange("p (c b t u) -> p c b t u", c=N_PASS, b=N_BATCH, t=P, u=2)
+        xc = const.tile([P, N_PASS * TOKENS], U32, name="xc", align_bytes=64)
+        xs = const.tile([P, N_PASS * TOKENS], U8, name="xs", align_bytes=64)
+        for b in range(N_BATCH):
+            xw = x_sb[b][:].bitcast(F32).rearrange("t (c p u) -> t c u p", c=N_PASS, p=P, u=2)
+            for ch in range(2):
+                xt = bank(2 * b + ch, [P, 2, 2, P], "xt")
+                for cc in range(2):
+                    for u in range(2):
+                        nc.tensor.transpose(xt[:, cc, u, :], xw[:, 2 * ch + cc, u, :], ident[:])
+                nc.vector.tensor_copy(
+                    out=gx_v[:, 2 * ch : 2 * ch + 2, b, :, :], in_=xt[:].rearrange("p c u t -> p c t u")
+                )
+        for ch in range(2):
+            nc.vector.quantize_mx(
+                out=xc[:, ch * 512 : (ch + 1) * 512].bitcast(FP8X4),
+                scales=xs[:, ch * 512 : (ch + 1) * 512],
+                in_=gx[:, ch * 2048 : (ch + 1) * 2048],
+            )
+
+        off = const.tile([P, HEADS * HEAD], F32, name="off")
+        rot = const.tile([P, HEADS * HEAD], F32, name="rot")
+        for h in range(HEADS):
+            cols = slice(h * HEAD, (h + 1) * HEAD)
+            nc.scalar.activation(out=off[:, cols], in_=swap[:], func=ACT.Copy, scale=sin_p[:, h : h + 1])
+            nc.vector.scalar_tensor_tensor(
+                out=rot[:, cols], in0=ident[:], scalar=trig[:, HEADS + h : HEADS + h + 1], in1=off[:, cols],
+                op0=ALU.mult, op1=ALU.add,
+            )
+
+        def regroup(copy, raw, grouped, j, lo, hi):
+            copy(
+                out=grouped[:, lo * PACK : hi * PACK].rearrange("p (c i t) -> p c t i", i=4, t=PACK),
+                in_=raw[:, :, j * CHUNK + lo : j * CHUNK + hi].rearrange("p t (c i) -> p c t i", i=4),
+            )
+
+        acc = {}
+        osb = {}
+        for m in range(3):
+            out_rows = [outs[m][b].rearrange("s h d -> s (h d)") for b in range(N_BATCH)]
+            for c in range(N_PASS):
+                raw = rawp.tile([P, PACK, DM], BF16, name="raw", tag="raw")
+                nc.sync.dma_start(
+                    out=raw[:],
+                    in_=weights[m][c * K_PASS : (c + 1) * K_PASS, :].rearrange("(p j) w -> p j w", j=PACK),
+                )
+                v_cols = V_COLS[m * N_PASS + c]
+                x_all = slice(c * TOKENS, (c + 1) * TOKENS)
+                for j in range(N_CHUNK):
+                    grouped = grpp.tile([P, CHUNK * PACK], BF16, name="grouped", tag="grouped", align_bytes=64)
+                    regroup(nc.vector.tensor_copy, raw, grouped, j, 0, v_cols)
+                    regroup(nc.scalar.copy, raw, grouped, j, v_cols, CHUNK)
+                    codes = codep.tile([P, CHUNK], U32, name="codes", tag="codes", align_bytes=64)
+                    scales = codep.tile([P, CHUNK], U8, name="scales", tag="scales", align_bytes=64)
+                    nc.vector.quantize_mx(out=codes[:].bitcast(FP8X4), scales=scales[:], in_=grouped[:])
+
+                    if m < 2:
+                        for i in range(2):
+                            if c == 0:
+                                acc[i] = acc.get(i, {})
+                                acc[i][j] = bank(2 * j + i, [P, 2 * TOKENS], "tq")
+                            for e in range(2):
+                                hh = 2 * i + e
+                                nc.tensor.matmul_mx(
+                                    out=acc[i][j][:, e * TOKENS : (e + 1) * TOKENS],
+                                    lhsT=codes[:, hh * HEAD : (hh + 1) * HEAD].bitcast(FP8X4),
+                                    lhsT_scale=scales[:, hh * HEAD : (hh + 1) * HEAD],
+                                    rhs=xc[:, x_all].bitcast(FP8X4),
+                                    rhs_scale=xs[:, x_all],
+                                    start=(c == 0 and e == 0),
+                                    stop=(c == N_PASS - 1 and e == 1),
+                                )
+                        if c == N_PASS - 1:
+                            tsb = []
+                            for i in range(2):
+                                ts = tsbp.tile([P, 2 * TOKENS], F32, name="tsb", tag="tsb")
+                                nc.scalar.copy(out=ts[:], in_=acc[i][j][:])
+                                tsb.append(ts)
+                            for b in range(N_BATCH):
+                                ob = bank(2 * j + b, [P, CHUNK], "ro")
+                                for hh in range(4):
+                                    lo = (hh % 2) * TOKENS + b * P
+                                    h = 4 * j + hh
+                                    nc.tensor.matmul(
+                                        out=ob[:, hh * HEAD : (hh + 1) * HEAD],
+                                        lhsT=tsb[hh // 2][:, lo : lo + P],
+                                        rhs=rot[:, h * HEAD : (h + 1) * HEAD],
+                                        start=True,
+                                        stop=True,
+                                    )
+                                if j % 2 == 0:
+                                    osb[b] = outp.tile([P, 2 * CHUNK], F32, name="osb", tag="osb")
+                                nc.scalar.copy(out=osb[b][:, (j % 2) * CHUNK : (j % 2 + 1) * CHUNK], in_=ob[:])
+                                if j % 2 == 1:
+                                    nc.scalar.dma_start(
+                                        out=out_rows[b][:, (j - 1) * CHUNK : (j + 1) * CHUNK], in_=osb[b][:]
+                                    )
+                    else:
+                        for b in range(N_BATCH):
+                            if c == 0:
+                                acc[b][j] = bank(2 * j + b, [P, CHUNK], "tv")
+                            x_b = slice(c * TOKENS + b * P, c * TOKENS + (b + 1) * P)
+                            nc.tensor.matmul_mx(
+                                out=acc[b][j][:],
+                                lhsT=xc[:, x_b].bitcast(FP8X4),
+                                lhsT_scale=xs[:, x_b],
+                                rhs=codes[:].bitcast(FP8X4),
+                                rhs_scale=scales[:],
+                                start=(c == 0),
+                                stop=(c == N_PASS - 1),
+                            )
+                        if c == N_PASS - 1:
+                            for b in range(N_BATCH):
+                                vsb = outp.tile([P, CHUNK], F32, name="vsb", tag="vsb")
+                                if b == 0:
+                                    nc.scalar.copy(out=vsb[:], in_=acc[b][j][:])
+                                    nc.scalar.dma_start(out=out_rows[b][:, j * CHUNK : (j + 1) * CHUNK], in_=vsb[:])
+                                else:
+                                    nc.vector.tensor_copy(out=vsb[:], in_=acc[b][j][:])
+                                    nc.sync.dma_start(out=out_rows[b][:, j * CHUNK : (j + 1) * CHUNK], in_=vsb[:])

@@ -25,10 +25,11 @@ CHUNK = 512
 N_CHUNK = DM // CHUNK
 TOKENS = N_BATCH * P
 ROPE_BASE = 10000.0
+PAIR_BITS = 6
 
 FLOPS = 2 * TOKENS * DM * 3 * DM
 
-V_COLS = (256, 256, 256, 256, 384, 384, 256, 256, 384, 384, 256, 256)
+V_COLS = (256, 256, 256, 288, 384, 384, 288, 288, 384, 384, 288, 256)
 
 
 def tile_selfattention_kernel(tc, x, Wq, Wk, Wv, st_pos, out_0, out_1, out_2):
@@ -54,37 +55,58 @@ def tile_selfattention_kernel(tc, x, Wq, Wk, Wv, st_pos, out_0, out_1, out_2):
             nc.sync.dma_start(out=xb[:], in_=x[b])
             x_sb.append(xb)
 
-        ident = const.tile([P, P], F32, name="ident")
-        make_identity(nc, ident[:])
         pidx_i = const.tile([P, 1], I32, name="pidx_i")
         nc.gpsimd.iota(pidx_i[:], pattern=[[0, 1]], base=0, channel_multiplier=1)
+        bitpos_i = const.tile([P, PAIR_BITS], I32, name="bitpos_i")
+        nc.gpsimd.iota(bitpos_i[:], pattern=[[1, PAIR_BITS]], base=1, channel_multiplier=0)
         hcol_i = const.tile([P, HEADS], I32, name="hcol_i")
         nc.gpsimd.iota(hcol_i[:], pattern=[[1, HEADS]], base=0, channel_multiplier=0)
+        ident = const.tile([P, P], F32, name="ident")
+        make_identity(nc, ident[:])
 
-        half_i = const.tile([P, 1], I32, name="half_i")
-        nc.vector.tensor_single_scalar(out=half_i[:], in_=pidx_i[:], scalar=1, op=ALU.arith_shift_right)
+        shifted_i = const.tile([P, PAIR_BITS], I32, name="shifted_i")
+        nc.vector.tensor_tensor(
+            out=shifted_i[:], in0=pidx_i[:, 0:1].to_broadcast([P, PAIR_BITS]), in1=bitpos_i[:],
+            op=ALU.logical_shift_right,
+        )
+        bit_i = const.tile([P, PAIR_BITS], I32, name="bit_i")
+        nc.vector.tensor_single_scalar(out=bit_i[:], in_=shifted_i[:], scalar=1, op=ALU.bitwise_and)
+        bit_f = const.tile([P, PAIR_BITS], F32, name="bit_f")
+        nc.vector.tensor_copy(out=bit_f[:], in_=bit_i[:])
+        factor1 = const.tile([P, PAIR_BITS], F32, name="factor1")
+        for j in range(PAIR_BITS):
+            nc.vector.tensor_scalar(
+                out=factor1[:, j : j + 1], in0=bit_f[:, j : j + 1],
+                scalar1=ROPE_BASE ** (-(2.0**j) / (HEAD // 2)) - 1.0, scalar2=1.0, op0=ALU.mult, op1=ALU.add,
+            )
+        prod3 = const.tile([P, 3], F32, name="prod3")
+        nc.vector.tensor_tensor(out=prod3[:], in0=factor1[:, 0:3], in1=factor1[:, 3:6], op=ALU.mult)
+        prod1 = const.tile([P, 1], F32, name="prod1")
+        nc.vector.tensor_tensor(out=prod1[:], in0=prod3[:, 0:1], in1=prod3[:, 1:2], op=ALU.mult)
+        phi = const.tile([P, 1], F32, name="phi")
+        nc.vector.scalar_tensor_tensor(
+            out=phi[:], in0=prod1[:], scalar=1.0 / (2.0 * math.pi), in1=prod3[:, 2:3], op0=ALU.mult, op1=ALU.mult
+        )
+
         par_i = const.tile([P, 1], I32, name="par_i")
         nc.vector.tensor_single_scalar(out=par_i[:], in_=pidx_i[:], scalar=1, op=ALU.bitwise_and)
-        half_f = const.tile([P, 1], F32, name="half_f")
-        nc.vector.tensor_copy(out=half_f[:], in_=half_i[:])
         par_f = const.tile([P, 1], F32, name="par_f")
         nc.vector.tensor_copy(out=par_f[:], in_=par_i[:])
-        hcol_f = const.tile([P, HEADS], F32, name="hcol_f")
-        nc.vector.tensor_copy(out=hcol_f[:], in_=hcol_i[:])
+        quarter = const.tile([P, 2], F32, name="quarter")
+        nc.vector.tensor_scalar(out=quarter[:, 0:1], in0=par_f[:], scalar1=-0.25, scalar2=0.25, op0=ALU.mult, op1=ALU.add)
+        nc.vector.tensor_scalar(out=quarter[:, 1:2], in0=par_f[:], scalar1=0.25, scalar2=None, op0=ALU.mult)
         sgn = const.tile([P, 1], F32, name="sgn")
         nc.vector.tensor_scalar(out=sgn[:], in0=par_f[:], scalar1=-2.0, scalar2=1.0, op0=ALU.mult, op1=ALU.add)
-
-        theta = const.tile([P, 1], F32, name="theta")
-        nc.scalar.activation(out=theta[:], in_=half_f[:], func=ACT.Exp, scale=-math.log(ROPE_BASE) / (HEAD // 2))
+        hcol_f = const.tile([P, HEADS], F32, name="hcol_f")
+        nc.vector.tensor_copy(out=hcol_f[:], in_=hcol_i[:])
 
         turns = const.tile([P, 2 * HEADS], F32, name="turns")
-        nc.vector.tensor_scalar(
-            out=turns[:, 0:HEADS], in0=hcol_f[:], scalar1=theta[:, 0:1], scalar2=1.0 / (2.0 * math.pi),
-            op0=ALU.mult, op1=ALU.mult,
-        )
-        nc.vector.tensor_scalar(
-            out=turns[:, HEADS : 2 * HEADS], in0=turns[:, 0:HEADS], scalar1=0.25, scalar2=None, op0=ALU.add
-        )
+        turns_v = turns[:].rearrange("p (h e) -> p h e", e=2)
+        for e in range(2):
+            nc.vector.tensor_scalar(
+                out=turns_v[:, :, e], in0=hcol_f[:], scalar1=phi[:, 0:1], scalar2=quarter[:, e : e + 1],
+                op0=ALU.mult, op1=ALU.add,
+            )
         red1 = const.tile([P, 2 * HEADS], F32, name="red1")
         nc.vector.scalar_tensor_tensor(out=red1[:], in0=turns[:], scalar=0.5, in1=turns[:], op0=ALU.is_gt, op1=ALU.subtract)
         red2 = const.tile([P, 2 * HEADS], F32, name="red2")
@@ -93,14 +115,23 @@ def tile_selfattention_kernel(tc, x, Wq, Wk, Wv, st_pos, out_0, out_1, out_2):
         nc.vector.scalar_tensor_tensor(out=red3[:], in0=turns[:], scalar=2.5, in1=red2[:], op0=ALU.is_gt, op1=ALU.add)
         trig = const.tile([P, 2 * HEADS], F32, name="trig")
         nc.scalar.activation(out=trig[:], in_=red3[:], func=ACT.Sin, scale=-2.0 * math.pi)
-        sin_p = const.tile([P, HEADS], F32, name="sin_p")
-        nc.vector.tensor_scalar(out=sin_p[:], in0=trig[:, 0:HEADS], scalar1=sgn[:, 0:1], scalar2=None, op0=ALU.mult)
+        trig_v = trig[:].rearrange("p (h e) -> p h e", e=2)
+        val = const.tile([P, 2 * HEADS], F32, name="val")
+        val_v = val[:].rearrange("p (h e) -> p h e", e=2)
+        nc.vector.tensor_scalar(out=val_v[:, :, 0], in0=trig_v[:, :, 0], scalar1=sgn[:, 0:1], scalar2=None, op0=ALU.mult)
+        nc.vector.tensor_copy(out=val_v[:, :, 1], in_=trig_v[:, :, 1])
 
-        swap = const.tile([P, P], F32, name="swap")
-        swap_v = swap[:].rearrange("p (i e) -> p i e", e=2)
         ident_v = ident[:].rearrange("p (i e) -> p i e", e=2)
-        nc.vector.tensor_copy(out=swap_v[:, :, 0], in_=ident_v[:, :, 1])
-        nc.vector.tensor_copy(out=swap_v[:, :, 1], in_=ident_v[:, :, 0])
+        pair = const.tile([P, HEAD // 2], F32, name="pair")
+        nc.vector.tensor_tensor(out=pair[:], in0=ident_v[:, :, 0], in1=ident_v[:, :, 1], op=ALU.add)
+        rot = const.tile([P, HEADS * HEAD], F32, name="rot")
+        rot_shape = [P, HEADS, HEAD // 2, 2]
+        nc.vector.tensor_tensor(
+            out=rot[:].rearrange("p (h i e) -> p h i e", h=HEADS, e=2),
+            in0=pair[:].unsqueeze(1).unsqueeze(3).to_broadcast(rot_shape),
+            in1=val_v.unsqueeze(2).to_broadcast(rot_shape),
+            op=ALU.mult,
+        )
 
         gx = const.tile([P, TOKENS * N_PASS * PACK], BF16, name="gx", align_bytes=64)
         gx_v = gx[:].bitcast(F32).rearrange("p (c b t u) -> p c b t u", c=N_PASS, b=N_BATCH, t=P, u=2)
@@ -113,7 +144,7 @@ def tile_selfattention_kernel(tc, x, Wq, Wk, Wv, st_pos, out_0, out_1, out_2):
                 for cc in range(2):
                     for u in range(2):
                         nc.tensor.transpose(xt[:, cc, u, :], xw[:, 2 * ch + cc, u, :], ident[:])
-                nc.vector.tensor_copy(
+                nc.scalar.copy(
                     out=gx_v[:, 2 * ch : 2 * ch + 2, b, :, :], in_=xt[:].rearrange("p c u t -> p c t u")
                 )
         for ch in range(2):
@@ -121,16 +152,6 @@ def tile_selfattention_kernel(tc, x, Wq, Wk, Wv, st_pos, out_0, out_1, out_2):
                 out=xc[:, ch * 512 : (ch + 1) * 512].bitcast(FP8X4),
                 scales=xs[:, ch * 512 : (ch + 1) * 512],
                 in_=gx[:, ch * 2048 : (ch + 1) * 2048],
-            )
-
-        off = const.tile([P, HEADS * HEAD], F32, name="off")
-        rot = const.tile([P, HEADS * HEAD], F32, name="rot")
-        for h in range(HEADS):
-            cols = slice(h * HEAD, (h + 1) * HEAD)
-            nc.scalar.activation(out=off[:, cols], in_=swap[:], func=ACT.Copy, scale=sin_p[:, h : h + 1])
-            nc.vector.scalar_tensor_tensor(
-                out=rot[:, cols], in0=ident[:], scalar=trig[:, HEADS + h : HEADS + h + 1], in1=off[:, cols],
-                op0=ALU.mult, op1=ALU.add,
             )
 
         def regroup(copy, raw, grouped, j, lo, hi):

@@ -29,7 +29,14 @@ PAIR_BITS = 6
 
 FLOPS = 2 * TOKENS * DM * 3 * DM
 
-V_COLS = (256, 256, 256, 288, 384, 384, 288, 288, 384, 384, 288, 256)
+N_UNITS = 3 * N_PASS * N_CHUNK
+LEAD = 2
+RAW_BUFS = 4
+V_COLS_BASE = 256
+V_COLS_STEP = 88
+TE_AFTER = 2
+ROT_EVERY = 2
+OE_AFTER = 4
 
 
 def tile_selfattention_kernel(tc, x, Wq, Wk, Wv, st_pos, out_0, out_1, out_2):
@@ -38,8 +45,9 @@ def tile_selfattention_kernel(tc, x, Wq, Wk, Wv, st_pos, out_0, out_1, out_2):
     outs = (out_0, out_1, out_2)
 
     with ExitStack() as ctx:
+        ctx.enter_context(tc.manual_schedule())
         const = ctx.enter_context(tc.tile_pool(name="const", bufs=1))
-        rawp = ctx.enter_context(tc.tile_pool(name="rawp", bufs=4))
+        rawp = ctx.enter_context(tc.tile_pool(name="rawp", bufs=RAW_BUFS))
         grpp = ctx.enter_context(tc.tile_pool(name="grpp", bufs=8))
         codep = ctx.enter_context(tc.tile_pool(name="codep", bufs=16))
         tsbp = ctx.enter_context(tc.tile_pool(name="tsbp", bufs=4))
@@ -147,6 +155,128 @@ def tile_selfattention_kernel(tc, x, Wq, Wk, Wv, st_pos, out_0, out_1, out_2):
                 nc.scalar.copy(
                     out=gx_v[:, 2 * ch : 2 * ch + 2, b, :, :], in_=xt[:].rearrange("p c u t -> p c t u")
                 )
+        out_rows = [[outs[m][b].rearrange("s h d -> s (h d)") for b in range(N_BATCH)] for m in range(3)]
+
+        plan = {}
+        for m in range(2):
+            first = (m * N_PASS + N_PASS - 1) * N_CHUNK
+            for j in range(N_CHUNK):
+                r_te = max(first + j + TE_AFTER, first + TE_AFTER + ROT_EVERY * j)
+                plan[r_te] = plan.get(r_te, []) + [("te", m, j)]
+                plan[r_te + OE_AFTER] = plan.get(r_te + OE_AFTER, []) + [("oe", m, j)]
+        for j in range(N_CHUNK):
+            r_ve = N_UNITS - N_CHUNK + j + 1
+            plan[r_ve] = plan.get(r_ve, []) + [("ve", 2, j)]
+
+        def v_cols_of(n):
+            banks_out = sum(1 if kind == "ve" else 2 for kind, m, j in plan.get(n - LEAD, []))
+            return min(CHUNK, V_COLS_BASE + V_COLS_STEP * banks_out)
+
+        raws = {}
+        groupeds = {}
+        codes = {}
+        scales = {}
+        acc = {}
+        tsb = {}
+        rotated = {}
+        osb = {}
+
+        def load(t):
+            raws[t] = rawp.tile([P, PACK, DM], BF16, name="raw", tag="raw")
+            m, c = divmod(t, N_PASS)
+            nc.sync.dma_start(
+                out=raws[t][:],
+                in_=weights[m][c * K_PASS : (c + 1) * K_PASS, :].rearrange("(p j) w -> p j w", j=PACK),
+            )
+
+        def regroup(copy, n, lo, hi):
+            if lo == hi:
+                return
+            t, j = divmod(n, N_CHUNK)
+            copy(
+                out=groupeds[n][:, lo * PACK : hi * PACK].rearrange("p (c i t) -> p c t i", i=4, t=PACK),
+                in_=raws[t][:, :, j * CHUNK + lo : j * CHUNK + hi].rearrange("p t (c i) -> p c t i", i=4),
+            )
+
+        def new_grouped(n):
+            groupeds[n] = grpp.tile([P, CHUNK * PACK], BF16, name="grouped", tag="grouped", align_bytes=64)
+
+        def quantise(n):
+            codes[n] = codep.tile([P, CHUNK], U32, name="codes", tag="codes", align_bytes=64)
+            scales[n] = codep.tile([P, CHUNK], U8, name="scales", tag="scales", align_bytes=64)
+            nc.vector.quantize_mx(out=codes[n][:].bitcast(FP8X4), scales=scales[n][:], in_=groupeds[n][:])
+
+        def multiply(n):
+            t, j = divmod(n, N_CHUNK)
+            m, c = divmod(t, N_PASS)
+            for i in range(2):
+                if c == 0:
+                    acc[(i, j)] = bank(2 * j + i, [P, CHUNK], "acc")
+                if m < 2:
+                    for e in range(2):
+                        hh = 2 * i + e
+                        nc.tensor.matmul_mx(
+                            out=acc[(i, j)][:, e * TOKENS : (e + 1) * TOKENS],
+                            lhsT=codes[n][:, hh * HEAD : (hh + 1) * HEAD].bitcast(FP8X4),
+                            lhsT_scale=scales[n][:, hh * HEAD : (hh + 1) * HEAD],
+                            rhs=xc[:, c * TOKENS : (c + 1) * TOKENS].bitcast(FP8X4),
+                            rhs_scale=xs[:, c * TOKENS : (c + 1) * TOKENS],
+                            start=(c == 0 and e == 0),
+                            stop=(c == N_PASS - 1 and e == 1),
+                        )
+                else:
+                    x_b = slice(c * TOKENS + i * P, c * TOKENS + (i + 1) * P)
+                    nc.tensor.matmul_mx(
+                        out=acc[(i, j)][:],
+                        lhsT=xc[:, x_b].bitcast(FP8X4),
+                        lhsT_scale=xs[:, x_b],
+                        rhs=codes[n][:].bitcast(FP8X4),
+                        rhs_scale=scales[n][:],
+                        start=(c == 0),
+                        stop=(c == N_PASS - 1),
+                    )
+
+        def sums_out_and_rotate(j):
+            for i in range(2):
+                tsb[i] = tsbp.tile([P, CHUNK], F32, name="tsb", tag="tsb")
+                nc.scalar.copy(out=tsb[i][:], in_=acc[(i, j)][:])
+            for b in range(N_BATCH):
+                rotated[(b, j)] = bank(2 * j + b, [P, CHUNK], "rotated")
+                for hh in range(4):
+                    lo = (hh % 2) * TOKENS + b * P
+                    h = 4 * j + hh
+                    nc.tensor.matmul(
+                        out=rotated[(b, j)][:, hh * HEAD : (hh + 1) * HEAD],
+                        lhsT=tsb[hh // 2][:, lo : lo + P],
+                        rhs=rot[:, h * HEAD : (h + 1) * HEAD],
+                        start=True,
+                        stop=True,
+                    )
+
+        def rotated_out(m, j):
+            for b in range(N_BATCH):
+                if j % 2 == 0:
+                    osb[b] = outp.tile([P, 2 * CHUNK], F32, name="osb", tag="osb")
+                nc.scalar.copy(out=osb[b][:, (j % 2) * CHUNK : (j % 2 + 1) * CHUNK], in_=rotated[(b, j)][:])
+                if j % 2 == 1:
+                    nc.scalar.dma_start(out=out_rows[m][b][:, (j - 1) * CHUNK : (j + 1) * CHUNK], in_=osb[b][:])
+
+        def v_out(j):
+            for b in range(N_BATCH):
+                vsb = outp.tile([P, CHUNK], F32, name="vsb", tag="vsb")
+                if b == 0:
+                    nc.scalar.copy(out=vsb[:], in_=acc[(b, j)][:])
+                    nc.scalar.dma_start(out=out_rows[2][b][:, j * CHUNK : (j + 1) * CHUNK], in_=vsb[:])
+                else:
+                    nc.vector.tensor_copy(out=vsb[:], in_=acc[(b, j)][:])
+                    nc.sync.dma_start(out=out_rows[2][b][:, j * CHUNK : (j + 1) * CHUNK], in_=vsb[:])
+
+        for t in range(RAW_BUFS):
+            load(t)
+        for n in range(LEAD):
+            new_grouped(n)
+            regroup(nc.vector.tensor_copy, n, 0, v_cols_of(n))
+            regroup(nc.scalar.copy, n, v_cols_of(n), CHUNK)
         for ch in range(2):
             nc.vector.quantize_mx(
                 out=xc[:, ch * 512 : (ch + 1) * 512].bitcast(FP8X4),
@@ -154,93 +284,37 @@ def tile_selfattention_kernel(tc, x, Wq, Wk, Wv, st_pos, out_0, out_1, out_2):
                 in_=gx[:, ch * 2048 : (ch + 1) * 2048],
             )
 
-        def regroup(copy, raw, grouped, j, lo, hi):
-            copy(
-                out=grouped[:, lo * PACK : hi * PACK].rearrange("p (c i t) -> p c t i", i=4, t=PACK),
-                in_=raw[:, :, j * CHUNK + lo : j * CHUNK + hi].rearrange("p t (c i) -> p c t i", i=4),
-            )
-
-        acc = {}
-        osb = {}
-        for m in range(3):
-            out_rows = [outs[m][b].rearrange("s h d -> s (h d)") for b in range(N_BATCH)]
-            for c in range(N_PASS):
-                raw = rawp.tile([P, PACK, DM], BF16, name="raw", tag="raw")
-                nc.sync.dma_start(
-                    out=raw[:],
-                    in_=weights[m][c * K_PASS : (c + 1) * K_PASS, :].rearrange("(p j) w -> p j w", j=PACK),
-                )
-                v_cols = V_COLS[m * N_PASS + c]
-                x_all = slice(c * TOKENS, (c + 1) * TOKENS)
-                for j in range(N_CHUNK):
-                    grouped = grpp.tile([P, CHUNK * PACK], BF16, name="grouped", tag="grouped", align_bytes=64)
-                    regroup(nc.vector.tensor_copy, raw, grouped, j, 0, v_cols)
-                    regroup(nc.scalar.copy, raw, grouped, j, v_cols, CHUNK)
-                    codes = codep.tile([P, CHUNK], U32, name="codes", tag="codes", align_bytes=64)
-                    scales = codep.tile([P, CHUNK], U8, name="scales", tag="scales", align_bytes=64)
-                    nc.vector.quantize_mx(out=codes[:].bitcast(FP8X4), scales=scales[:], in_=grouped[:])
-
-                    if m < 2:
-                        for i in range(2):
-                            if c == 0:
-                                acc[i] = acc.get(i, {})
-                                acc[i][j] = bank(2 * j + i, [P, 2 * TOKENS], "tq")
-                            for e in range(2):
-                                hh = 2 * i + e
-                                nc.tensor.matmul_mx(
-                                    out=acc[i][j][:, e * TOKENS : (e + 1) * TOKENS],
-                                    lhsT=codes[:, hh * HEAD : (hh + 1) * HEAD].bitcast(FP8X4),
-                                    lhsT_scale=scales[:, hh * HEAD : (hh + 1) * HEAD],
-                                    rhs=xc[:, x_all].bitcast(FP8X4),
-                                    rhs_scale=xs[:, x_all],
-                                    start=(c == 0 and e == 0),
-                                    stop=(c == N_PASS - 1 and e == 1),
-                                )
-                        if c == N_PASS - 1:
-                            tsb = []
-                            for i in range(2):
-                                ts = tsbp.tile([P, 2 * TOKENS], F32, name="tsb", tag="tsb")
-                                nc.scalar.copy(out=ts[:], in_=acc[i][j][:])
-                                tsb.append(ts)
-                            for b in range(N_BATCH):
-                                ob = bank(2 * j + b, [P, CHUNK], "ro")
-                                for hh in range(4):
-                                    lo = (hh % 2) * TOKENS + b * P
-                                    h = 4 * j + hh
-                                    nc.tensor.matmul(
-                                        out=ob[:, hh * HEAD : (hh + 1) * HEAD],
-                                        lhsT=tsb[hh // 2][:, lo : lo + P],
-                                        rhs=rot[:, h * HEAD : (h + 1) * HEAD],
-                                        start=True,
-                                        stop=True,
-                                    )
-                                if j % 2 == 0:
-                                    osb[b] = outp.tile([P, 2 * CHUNK], F32, name="osb", tag="osb")
-                                nc.scalar.copy(out=osb[b][:, (j % 2) * CHUNK : (j % 2 + 1) * CHUNK], in_=ob[:])
-                                if j % 2 == 1:
-                                    nc.scalar.dma_start(
-                                        out=out_rows[b][:, (j - 1) * CHUNK : (j + 1) * CHUNK], in_=osb[b][:]
-                                    )
-                    else:
-                        for b in range(N_BATCH):
-                            if c == 0:
-                                acc[b][j] = bank(2 * j + b, [P, CHUNK], "tv")
-                            x_b = slice(c * TOKENS + b * P, c * TOKENS + (b + 1) * P)
-                            nc.tensor.matmul_mx(
-                                out=acc[b][j][:],
-                                lhsT=xc[:, x_b].bitcast(FP8X4),
-                                lhsT_scale=xs[:, x_b],
-                                rhs=codes[:].bitcast(FP8X4),
-                                rhs_scale=scales[:],
-                                start=(c == 0),
-                                stop=(c == N_PASS - 1),
-                            )
-                        if c == N_PASS - 1:
-                            for b in range(N_BATCH):
-                                vsb = outp.tile([P, CHUNK], F32, name="vsb", tag="vsb")
-                                if b == 0:
-                                    nc.scalar.copy(out=vsb[:], in_=acc[b][j][:])
-                                    nc.scalar.dma_start(out=out_rows[b][:, j * CHUNK : (j + 1) * CHUNK], in_=vsb[:])
-                                else:
-                                    nc.vector.tensor_copy(out=vsb[:], in_=acc[b][j][:])
-                                    nc.sync.dma_start(out=out_rows[b][:, j * CHUNK : (j + 1) * CHUNK], in_=vsb[:])
+        waiting = []
+        held = [False] * N_CHUNK
+        for r in range(N_UNITS + TE_AFTER + ROT_EVERY * N_CHUNK + OE_AFTER):
+            for kind, m, j in plan.get(r, []):
+                if kind == "te":
+                    sums_out_and_rotate(j)
+                elif kind == "oe":
+                    rotated_out(m, j)
+                    held[j] = False
+                else:
+                    v_out(j)
+            if r < N_UNITS:
+                ahead = r + LEAD
+                if ahead < N_UNITS:
+                    new_grouped(ahead)
+                    regroup(nc.scalar.copy, ahead, v_cols_of(ahead), CHUNK)
+                quantise(r)
+                if ahead < N_UNITS:
+                    regroup(nc.vector.tensor_copy, ahead, 0, v_cols_of(ahead))
+                    if ahead % N_CHUNK == N_CHUNK - 1 and ahead // N_CHUNK + RAW_BUFS < 3 * N_PASS:
+                        load(ahead // N_CHUNK + RAW_BUFS)
+                waiting.append(r)
+            still = []
+            for n in waiting:
+                t, j = divmod(n, N_CHUNK)
+                m, c = divmod(t, N_PASS)
+                if (c == 0 and held[j]) or any(w % N_CHUNK == j for w in still):
+                    still.append(n)
+                else:
+                    multiply(n)
+                    if c == N_PASS - 1 and m < 2:
+                        held[j] = True
+            waiting = still
+        assert not waiting

@@ -52,6 +52,7 @@ def tile_selfattention_kernel(tc, x, Wq, Wk, Wv, st_pos, out_0, out_1, out_2):
         codep = ctx.enter_context(tc.tile_pool(name="codep", bufs=16))
         tsbp = ctx.enter_context(tc.tile_pool(name="tsbp", bufs=4))
         outp = ctx.enter_context(tc.tile_pool(name="outp", bufs=4))
+        vout = ctx.enter_context(tc.tile_pool(name="vout", bufs=2 * N_CHUNK))
         psum = ctx.enter_context(tc.psum_pool(name="psum", bufs=1))
 
         def bank(i, shape, label):
@@ -168,8 +169,14 @@ def tile_selfattention_kernel(tc, x, Wq, Wk, Wv, st_pos, out_0, out_1, out_2):
             r_ve = N_UNITS - N_CHUNK + j + 1
             plan[r_ve] = plan.get(r_ve, []) + [("ve", 2, j)]
 
+        def on_vector(j, b):
+            return j == N_CHUNK - 1 and b == N_BATCH - 1
+
         def v_cols_of(n):
-            banks_out = sum(1 if kind == "ve" else 2 for kind, m, j in plan.get(n - LEAD, []))
+            banks_out = sum(
+                sum(1 for b in range(N_BATCH) if kind != "ve" or not on_vector(j, b))
+                for kind, m, j in plan.get(n - LEAD, [])
+            )
             return min(CHUNK, V_COLS_BASE + V_COLS_STEP * banks_out)
 
         raws = {}
@@ -263,8 +270,8 @@ def tile_selfattention_kernel(tc, x, Wq, Wk, Wv, st_pos, out_0, out_1, out_2):
 
         def v_out(j):
             for b in range(N_BATCH):
-                vsb = outp.tile([P, CHUNK], F32, name="vsb", tag="vsb")
-                if b == 0:
+                vsb = vout.tile([P, CHUNK], F32, name="vsb", tag="vsb")
+                if not on_vector(j, b):
                     nc.scalar.copy(out=vsb[:], in_=acc[(b, j)][:])
                     nc.scalar.dma_start(out=out_rows[2][b][:, j * CHUNK : (j + 1) * CHUNK], in_=vsb[:])
                 else:

@@ -29,14 +29,19 @@ PAIR_BITS = 6
 
 FLOPS = 2 * TOKENS * DM * 3 * DM
 
-N_UNITS = 3 * N_PASS * N_CHUNK
+N_SLABS = 3 * N_PASS
+WIDE = 2 * CHUNK
+UNITS = [(t, c0, WIDE) for t in range(N_SLABS - 1) for c0 in range(0, DM, WIDE)] + [
+    (N_SLABS - 1, c0, CHUNK) for c0 in range(0, DM, CHUNK)
+]
+N_UNITS = len(UNITS)
 LEAD = 2
 RAW_BUFS = 4
-V_COLS_BASE = 256
+V_COLS_BASE = 248
 V_COLS_STEP = 88
-TE_AFTER = 2
-ROT_EVERY = 2
-OE_AFTER = 4
+TE_AFTER = 1
+ROT_EVERY = 1
+OE_AFTER = 2
 
 
 def tile_selfattention_kernel(tc, x, Wq, Wk, Wv, st_pos, out_0, out_1, out_2):
@@ -48,8 +53,8 @@ def tile_selfattention_kernel(tc, x, Wq, Wk, Wv, st_pos, out_0, out_1, out_2):
         ctx.enter_context(tc.manual_schedule())
         const = ctx.enter_context(tc.tile_pool(name="const", bufs=1))
         rawp = ctx.enter_context(tc.tile_pool(name="rawp", bufs=RAW_BUFS))
-        grpp = ctx.enter_context(tc.tile_pool(name="grpp", bufs=8))
-        codep = ctx.enter_context(tc.tile_pool(name="codep", bufs=16))
+        grpp = ctx.enter_context(tc.tile_pool(name="grpp", bufs=5))
+        codep = ctx.enter_context(tc.tile_pool(name="codep", bufs=8))
         tsbp = ctx.enter_context(tc.tile_pool(name="tsbp", bufs=4))
         outp = ctx.enter_context(tc.tile_pool(name="outp", bufs=4))
         vout = ctx.enter_context(tc.tile_pool(name="vout", bufs=2 * N_CHUNK))
@@ -158,26 +163,35 @@ def tile_selfattention_kernel(tc, x, Wq, Wk, Wv, st_pos, out_0, out_1, out_2):
                 )
         out_rows = [[outs[m][b].rearrange("s h d -> s (h d)") for b in range(N_BATCH)] for m in range(3)]
 
-        plan = {}
-        for m in range(2):
-            first = (m * N_PASS + N_PASS - 1) * N_CHUNK
-            for j in range(N_CHUNK):
-                r_te = max(first + j + TE_AFTER, first + TE_AFTER + ROT_EVERY * j)
-                plan[r_te] = plan.get(r_te, []) + [("te", m, j)]
-                plan[r_te + OE_AFTER] = plan.get(r_te + OE_AFTER, []) + [("oe", m, j)]
-        for j in range(N_CHUNK):
-            r_ve = N_UNITS - N_CHUNK + j + 1
-            plan[r_ve] = plan.get(r_ve, []) + [("ve", 2, j)]
+        def chunks_of(n):
+            t, c0, width = UNITS[n]
+            return range(c0 // CHUNK, (c0 + width) // CHUNK)
+
+        def last_unit(m, j):
+            return max(n for n in range(N_UNITS) if UNITS[n][0] == m * N_PASS + N_PASS - 1 and j in chunks_of(n))
 
         def on_vector(j, b):
             return j == N_CHUNK - 1 and b == N_BATCH - 1
+
+        plan = {}
+        for m in range(2):
+            r_te = -ROT_EVERY
+            for j in range(N_CHUNK):
+                r_te = max(last_unit(m, j) + TE_AFTER, r_te + ROT_EVERY)
+                plan[r_te] = plan.get(r_te, []) + [("te", m, j)]
+                plan[r_te + OE_AFTER] = plan.get(r_te + OE_AFTER, []) + [("oe", m, j)]
+        for j in range(N_CHUNK):
+            r_ve = last_unit(2, j) + 1
+            plan[r_ve] = plan.get(r_ve, []) + [("ve", 2, j)]
+        n_rounds = max(plan) + 1
 
         def v_cols_of(n):
             banks_out = sum(
                 sum(1 for b in range(N_BATCH) if kind != "ve" or not on_vector(j, b))
                 for kind, m, j in plan.get(n - LEAD, [])
             )
-            return min(CHUNK, V_COLS_BASE + V_COLS_STEP * banks_out)
+            width = UNITS[n][2]
+            return min(width, V_COLS_BASE * width // CHUNK + V_COLS_STEP * banks_out)
 
         raws = {}
         groupeds = {}
@@ -196,36 +210,49 @@ def tile_selfattention_kernel(tc, x, Wq, Wk, Wv, st_pos, out_0, out_1, out_2):
                 in_=weights[m][c * K_PASS : (c + 1) * K_PASS, :].rearrange("(p j) w -> p j w", j=PACK),
             )
 
+        def load_next(n):
+            t, c0, width = UNITS[n]
+            if c0 + width == DM and t + RAW_BUFS < N_SLABS:
+                load(t + RAW_BUFS)
+
         def regroup(copy, n, lo, hi):
             if lo == hi:
                 return
-            t, j = divmod(n, N_CHUNK)
+            t, c0, width = UNITS[n]
             copy(
                 out=groupeds[n][:, lo * PACK : hi * PACK].rearrange("p (c i t) -> p c t i", i=4, t=PACK),
-                in_=raws[t][:, :, j * CHUNK + lo : j * CHUNK + hi].rearrange("p t (c i) -> p c t i", i=4),
+                in_=raws[t][:, :, c0 + lo : c0 + hi].rearrange("p t (c i) -> p c t i", i=4),
             )
 
+        def scalar_cut(n):
+            lo, hi = v_cols_of(n), UNITS[n][2]
+            if not any(kind == "oe" for kind, m, j in plan.get(n - LEAD, [])):
+                return hi
+            return lo + (hi - lo) // 16 * 8
+
         def new_grouped(n):
-            groupeds[n] = grpp.tile([P, CHUNK * PACK], BF16, name="grouped", tag="grouped", align_bytes=64)
+            groupeds[n] = grpp.tile([P, UNITS[n][2] * PACK], BF16, name="grouped", tag="grouped", align_bytes=64)
 
         def quantise(n):
-            codes[n] = codep.tile([P, CHUNK], U32, name="codes", tag="codes", align_bytes=64)
-            scales[n] = codep.tile([P, CHUNK], U8, name="scales", tag="scales", align_bytes=64)
+            width = UNITS[n][2]
+            codes[n] = codep.tile([P, width], U32, name="codes", tag="codes", align_bytes=64)
+            scales[n] = codep.tile([P, width], U8, name="scales", tag="scales", align_bytes=64)
             nc.vector.quantize_mx(out=codes[n][:].bitcast(FP8X4), scales=scales[n][:], in_=groupeds[n][:])
 
-        def multiply(n):
-            t, j = divmod(n, N_CHUNK)
+        def multiply(n, j):
+            t, c0, width = UNITS[n]
             m, c = divmod(t, N_PASS)
+            at = j * CHUNK - c0
             for i in range(2):
                 if c == 0:
                     acc[(i, j)] = bank(2 * j + i, [P, CHUNK], "acc")
                 if m < 2:
                     for e in range(2):
-                        hh = 2 * i + e
+                        w_cols = slice(at + (2 * i + e) * HEAD, at + (2 * i + e + 1) * HEAD)
                         nc.tensor.matmul_mx(
                             out=acc[(i, j)][:, e * TOKENS : (e + 1) * TOKENS],
-                            lhsT=codes[n][:, hh * HEAD : (hh + 1) * HEAD].bitcast(FP8X4),
-                            lhsT_scale=scales[n][:, hh * HEAD : (hh + 1) * HEAD],
+                            lhsT=codes[n][:, w_cols].bitcast(FP8X4),
+                            lhsT_scale=scales[n][:, w_cols],
                             rhs=xc[:, c * TOKENS : (c + 1) * TOKENS].bitcast(FP8X4),
                             rhs_scale=xs[:, c * TOKENS : (c + 1) * TOKENS],
                             start=(c == 0 and e == 0),
@@ -237,8 +264,8 @@ def tile_selfattention_kernel(tc, x, Wq, Wk, Wv, st_pos, out_0, out_1, out_2):
                         out=acc[(i, j)][:],
                         lhsT=xc[:, x_b].bitcast(FP8X4),
                         lhsT_scale=xs[:, x_b],
-                        rhs=codes[n][:].bitcast(FP8X4),
-                        rhs_scale=scales[n][:],
+                        rhs=codes[n][:, at : at + CHUNK].bitcast(FP8X4),
+                        rhs_scale=scales[n][:, at : at + CHUNK],
                         start=(c == 0),
                         stop=(c == N_PASS - 1),
                     )
@@ -266,61 +293,62 @@ def tile_selfattention_kernel(tc, x, Wq, Wk, Wv, st_pos, out_0, out_1, out_2):
                     osb[b] = outp.tile([P, 2 * CHUNK], F32, name="osb", tag="osb")
                 nc.scalar.copy(out=osb[b][:, (j % 2) * CHUNK : (j % 2 + 1) * CHUNK], in_=rotated[(b, j)][:])
                 if j % 2 == 1:
-                    nc.scalar.dma_start(out=out_rows[m][b][:, (j - 1) * CHUNK : (j + 1) * CHUNK], in_=osb[b][:])
+                    nc.sync.dma_start(out=out_rows[m][b][:, (j - 1) * CHUNK : (j + 1) * CHUNK], in_=osb[b][:])
 
         def v_out(j):
             for b in range(N_BATCH):
                 vsb = vout.tile([P, CHUNK], F32, name="vsb", tag="vsb")
-                if not on_vector(j, b):
-                    nc.scalar.copy(out=vsb[:], in_=acc[(b, j)][:])
-                    nc.scalar.dma_start(out=out_rows[2][b][:, j * CHUNK : (j + 1) * CHUNK], in_=vsb[:])
-                else:
+                if on_vector(j, b):
                     nc.vector.tensor_copy(out=vsb[:], in_=acc[(b, j)][:])
-                    nc.sync.dma_start(out=out_rows[2][b][:, j * CHUNK : (j + 1) * CHUNK], in_=vsb[:])
+                else:
+                    nc.scalar.copy(out=vsb[:], in_=acc[(b, j)][:])
+                nc.sync.dma_start(out=out_rows[2][b][:, j * CHUNK : (j + 1) * CHUNK], in_=vsb[:])
 
         for t in range(RAW_BUFS):
             load(t)
-        for n in range(LEAD):
-            new_grouped(n)
-            regroup(nc.vector.tensor_copy, n, 0, v_cols_of(n))
-            regroup(nc.scalar.copy, n, v_cols_of(n), CHUNK)
         for ch in range(2):
             nc.vector.quantize_mx(
                 out=xc[:, ch * 512 : (ch + 1) * 512].bitcast(FP8X4),
                 scales=xs[:, ch * 512 : (ch + 1) * 512],
                 in_=gx[:, ch * 2048 : (ch + 1) * 2048],
             )
+        for n in range(LEAD):
+            new_grouped(n)
+            regroup(nc.vector.tensor_copy, n, 0, v_cols_of(n))
+            regroup(nc.scalar.copy, n, v_cols_of(n), UNITS[n][2])
+            load_next(n)
 
         waiting = []
         held = [False] * N_CHUNK
-        for r in range(N_UNITS + TE_AFTER + ROT_EVERY * N_CHUNK + OE_AFTER):
+        for r in range(n_rounds):
+            ahead = r + LEAD
             for kind, m, j in plan.get(r, []):
                 if kind == "te":
                     sums_out_and_rotate(j)
-                elif kind == "oe":
+                elif kind == "ve":
+                    v_out(j)
+            if ahead < N_UNITS:
+                new_grouped(ahead)
+                regroup(nc.scalar.copy, ahead, v_cols_of(ahead), scalar_cut(ahead))
+            for kind, m, j in plan.get(r, []):
+                if kind == "oe":
                     rotated_out(m, j)
                     held[j] = False
-                else:
-                    v_out(j)
+            if ahead < N_UNITS:
+                regroup(nc.scalar.copy, ahead, scalar_cut(ahead), UNITS[ahead][2])
             if r < N_UNITS:
-                ahead = r + LEAD
-                if ahead < N_UNITS:
-                    new_grouped(ahead)
-                    regroup(nc.scalar.copy, ahead, v_cols_of(ahead), CHUNK)
                 quantise(r)
-                if ahead < N_UNITS:
-                    regroup(nc.vector.tensor_copy, ahead, 0, v_cols_of(ahead))
-                    if ahead % N_CHUNK == N_CHUNK - 1 and ahead // N_CHUNK + RAW_BUFS < 3 * N_PASS:
-                        load(ahead // N_CHUNK + RAW_BUFS)
-                waiting.append(r)
+                waiting.extend((r, j) for j in chunks_of(r))
+            if ahead < N_UNITS:
+                regroup(nc.vector.tensor_copy, ahead, 0, v_cols_of(ahead))
+                load_next(ahead)
             still = []
-            for n in waiting:
-                t, j = divmod(n, N_CHUNK)
-                m, c = divmod(t, N_PASS)
-                if (c == 0 and held[j]) or any(w % N_CHUNK == j for w in still):
-                    still.append(n)
+            for n, j in waiting:
+                m, c = divmod(UNITS[n][0], N_PASS)
+                if (c == 0 and held[j]) or any(w[1] == j for w in still):
+                    still.append((n, j))
                 else:
-                    multiply(n)
+                    multiply(n, j)
                     if c == N_PASS - 1 and m < 2:
                         held[j] = True
             waiting = still

@@ -37,11 +37,11 @@ UNITS = [(t, c0, WIDE) for t in range(N_SLABS - 1) for c0 in range(0, DM, WIDE)]
 N_UNITS = len(UNITS)
 LEAD = 2
 RAW_BUFS = 4
-V_COLS_BASE = 248
-V_COLS_STEP = 88
+V_COLS_BASE = 256
+V_COLS_STEP = 72
 TE_AFTER = 1
 ROT_EVERY = 1
-OE_AFTER = 2
+OE_AFTER = 1
 
 
 def tile_selfattention_kernel(tc, x, Wq, Wk, Wv, st_pos, out_0, out_1, out_2):

@@ -35,6 +35,7 @@ UNITS = [(t, c0, WIDE) for t in range(N_SLABS - 1) for c0 in range(0, DM, WIDE)]
     (N_SLABS - 1, c0, CHUNK) for c0 in range(0, DM, CHUNK)
 ]
 N_UNITS = len(UNITS)
+RUN = 8
 LEAD = 2
 RAW_BUFS = 4
 V_COLS_BASE = 256
@@ -220,8 +221,8 @@ def tile_selfattention_kernel(tc, x, Wq, Wk, Wv, st_pos, out_0, out_1, out_2):
                 return
             t, c0, width = UNITS[n]
             copy(
-                out=groupeds[n][:, lo * PACK : hi * PACK].rearrange("p (c i t) -> p c t i", i=4, t=PACK),
-                in_=raws[t][:, :, c0 + lo : c0 + hi].rearrange("p t (c i) -> p c t i", i=4),
+                out=groupeds[n][:, lo * PACK : hi * PACK].rearrange("p (c i t) -> p c t i", i=RUN, t=PACK),
+                in_=raws[t][:, :, c0 + lo : c0 + hi].rearrange("p t (c i) -> p c t i", i=RUN),
             )
 
         def scalar_cut(n):

@@ -221,8 +221,8 @@ def tile_selfattention_kernel(tc, x, Wq, Wk, Wv, st_pos, out_0, out_1, out_2):
                 return
             t, c0, width = UNITS[n]
             copy(
-                out=groupeds[n][:, lo * PACK : hi * PACK].rearrange("p (c i t) -> p c t i", i=RUN, t=PACK),
-                in_=raws[t][:, :, c0 + lo : c0 + hi].rearrange("p t (c i) -> p c t i", i=RUN),
+                out=groupeds[n][:, lo * PACK : hi * PACK].rearrange("p (c i u v) -> p c u i v", i=RUN, u=2, v=2),
+                in_=raws[t][:, :, c0 + lo : c0 + hi].rearrange("p (u v) (c i) -> p c u i v", u=2, i=RUN),
             )
 
         def scalar_cut(n):

@@ -31,8 +31,12 @@ FLOPS = 2 * TOKENS * DM * 3 * DM
 
 N_SLABS = 3 * N_PASS
 WIDE = 2 * CHUNK
-UNITS = [(t, c0, WIDE) for t in range(N_SLABS - 1) for c0 in range(0, DM, WIDE)] + [
-    (N_SLABS - 1, c0, CHUNK) for c0 in range(0, DM, CHUNK)
+UNITS = [(t, c0, WIDE) for t in range(N_SLABS - 2) for c0 in range(0, DM, WIDE)] + [
+    (N_SLABS - 2, 0, WIDE),
+    (N_SLABS - 1, 0, WIDE),
+    (N_SLABS - 2, WIDE, WIDE),
+    (N_SLABS - 1, WIDE, CHUNK),
+    (N_SLABS - 1, WIDE + CHUNK, CHUNK),
 ]
 N_UNITS = len(UNITS)
 RUN = 8
@@ -172,7 +176,7 @@ def tile_selfattention_kernel(tc, x, Wq, Wk, Wv, st_pos, out_0, out_1, out_2):
             return max(n for n in range(N_UNITS) if UNITS[n][0] == m * N_PASS + N_PASS - 1 and j in chunks_of(n))
 
         def on_vector(j, b):
-            return j == N_CHUNK - 1 and b == N_BATCH - 1
+            return j >= N_CHUNK - 2 and b == N_BATCH - 1
 
         plan = {}
         for m in range(2):
@@ -182,7 +186,7 @@ def tile_selfattention_kernel(tc, x, Wq, Wk, Wv, st_pos, out_0, out_1, out_2):
                 plan[r_te] = plan.get(r_te, []) + [("te", m, j)]
                 plan[r_te + OE_AFTER] = plan.get(r_te + OE_AFTER, []) + [("oe", m, j)]
         for j in range(N_CHUNK):
-            r_ve = last_unit(2, j) + 1
+            r_ve = last_unit(2, j) + 1 + (1 if j == 1 else 0)
             plan[r_ve] = plan.get(r_ve, []) + [("ve", 2, j)]
         n_rounds = max(plan) + 1
 
@@ -296,10 +300,12 @@ def tile_selfattention_kernel(tc, x, Wq, Wk, Wv, st_pos, out_0, out_1, out_2):
                 if j % 2 == 1:
                     nc.sync.dma_start(out=out_rows[m][b][:, (j - 1) * CHUNK : (j + 1) * CHUNK], in_=osb[b][:])
 
-        def v_out(j):
+        def v_out(j, by_vector):
             for b in range(N_BATCH):
+                if on_vector(j, b) != by_vector:
+                    continue
                 vsb = vout.tile([P, CHUNK], F32, name="vsb", tag="vsb")
-                if on_vector(j, b):
+                if by_vector:
                     nc.vector.tensor_copy(out=vsb[:], in_=acc[(b, j)][:])
                 else:
                     nc.scalar.copy(out=vsb[:], in_=acc[(b, j)][:])
@@ -327,7 +333,7 @@ def tile_selfattention_kernel(tc, x, Wq, Wk, Wv, st_pos, out_0, out_1, out_2):
                 if kind == "te":
                     sums_out_and_rotate(j)
                 elif kind == "ve":
-                    v_out(j)
+                    v_out(j, False)
             if ahead < N_UNITS:
                 new_grouped(ahead)
                 regroup(nc.scalar.copy, ahead, v_cols_of(ahead), scalar_cut(ahead))
@@ -343,6 +349,9 @@ def tile_selfattention_kernel(tc, x, Wq, Wk, Wv, st_pos, out_0, out_1, out_2):
             if ahead < N_UNITS:
                 regroup(nc.vector.tensor_copy, ahead, 0, v_cols_of(ahead))
                 load_next(ahead)
+            for kind, m, j in plan.get(r, []):
+                if kind == "ve":
+                    v_out(j, True)
             still = []
             for n, j in waiting:
                 m, c = divmod(UNITS[n][0], N_PASS)

import math
from contextlib import ExitStack

import concourse.mybir as mybir
from concourse.masks import make_identity

F32 = mybir.dt.float32
BF16 = mybir.dt.bfloat16
U32 = mybir.dt.uint32
U8 = mybir.dt.uint8
I32 = mybir.dt.int32
FP8X4 = mybir.dt.float8_e4m3fn_x4
ALU = mybir.AluOpType
ACT = mybir.ActivationFunctionType

P = 128
N_BATCH = 2
DM = 2048
HEADS = 16
HEAD = 128
PACK = 4
K_PASS = P * PACK
N_PASS = DM // K_PASS
CHUNK = 512
N_CHUNK = DM // CHUNK
TOKENS = N_BATCH * P
ROPE_BASE = 10000.0
PAIR_BITS = 6

FLOPS = 2 * TOKENS * DM * 3 * DM

N_SLABS = 3 * N_PASS
WIDE = 2 * CHUNK
UNITS = [(t, c0, WIDE) for t in range(N_SLABS - 2) for c0 in range(0, DM, WIDE)] + [
    (N_SLABS - 2, 0, WIDE),
    (N_SLABS - 1, 0, WIDE),
    (N_SLABS - 2, WIDE, WIDE),
    (N_SLABS - 1, WIDE, CHUNK),
    (N_SLABS - 1, WIDE + CHUNK, CHUNK),
]
N_UNITS = len(UNITS)
RUN = 8
LEAD = 2
RAW_BUFS = 4
V_COLS_BASE = 256
V_COLS_STEP = 72
TE_AFTER = 1
ROT_EVERY = 1
OE_AFTER = 1


def tile_selfattention_kernel(tc, x, Wq, Wk, Wv, st_pos, out_0, out_1, out_2):
    nc = tc.nc
    weights = (Wq, Wk, Wv)
    outs = (out_0, out_1, out_2)

    with ExitStack() as ctx:
        ctx.enter_context(tc.manual_schedule())
        const = ctx.enter_context(tc.tile_pool(name="const", bufs=1))
        rawp = ctx.enter_context(tc.tile_pool(name="rawp", bufs=RAW_BUFS))
        grpp = ctx.enter_context(tc.tile_pool(name="grpp", bufs=5))
        codep = ctx.enter_context(tc.tile_pool(name="codep", bufs=8))
        tsbp = ctx.enter_context(tc.tile_pool(name="tsbp", bufs=4))
        outp = ctx.enter_context(tc.tile_pool(name="outp", bufs=4))
        vout = ctx.enter_context(tc.tile_pool(name="vout", bufs=2 * N_CHUNK))
        psum = ctx.enter_context(tc.psum_pool(name="psum", bufs=1))

        def bank(i, shape, label):
            return psum.tile(shape, F32, name="%s%d" % (label, i), tag="bank%d" % i)

        x_sb = []
        for b in range(N_BATCH):
            xb = const.tile([P, DM], BF16, name="x_sb%d" % b)
            nc.sync.dma_start(out=xb[:], in_=x[b])
            x_sb.append(xb)

        pidx_i = const.tile([P, 1], I32, name="pidx_i")
        nc.gpsimd.iota(pidx_i[:], pattern=[[0, 1]], base=0, channel_multiplier=1)
        bitpos_i = const.tile([P, PAIR_BITS], I32, name="bitpos_i")
        nc.gpsimd.iota(bitpos_i[:], pattern=[[1, PAIR_BITS]], base=1, channel_multiplier=0)
        hcol_i = const.tile([P, HEADS], I32, name="hcol_i")
        nc.gpsimd.iota(hcol_i[:], pattern=[[1, HEADS]], base=0, channel_multiplier=0)
        ident = const.tile([P, P], F32, name="ident")
        make_identity(nc, ident[:])

        shifted_i = const.tile([P, PAIR_BITS], I32, name="shifted_i")
        nc.vector.tensor_tensor(
            out=shifted_i[:], in0=pidx_i[:, 0:1].to_broadcast([P, PAIR_BITS]), in1=bitpos_i[:],
            op=ALU.logical_shift_right,
        )
        bit_i = const.tile([P, PAIR_BITS], I32, name="bit_i")
        nc.vector.tensor_single_scalar(out=bit_i[:], in_=shifted_i[:], scalar=1, op=ALU.bitwise_and)
        bit_f = const.tile([P, PAIR_BITS], F32, name="bit_f")
        nc.vector.tensor_copy(out=bit_f[:], in_=bit_i[:])
        factor1 = const.tile([P, PAIR_BITS], F32, name="factor1")
        for j in range(PAIR_BITS):
            nc.vector.tensor_scalar(
                out=factor1[:, j : j + 1], in0=bit_f[:, j : j + 1],
                scalar1=ROPE_BASE ** (-(2.0**j) / (HEAD // 2)) - 1.0, scalar2=1.0, op0=ALU.mult, op1=ALU.add,
            )
        prod3 = const.tile([P, 3], F32, name="prod3")
        nc.vector.tensor_tensor(out=prod3[:], in0=factor1[:, 0:3], in1=factor1[:, 3:6], op=ALU.mult)
        prod1 = const.tile([P, 1], F32, name="prod1")
        nc.vector.tensor_tensor(out=prod1[:], in0=prod3[:, 0:1], in1=prod3[:, 1:2], op=ALU.mult)
        phi = const.tile([P, 1], F32, name="phi")
        nc.vector.scalar_tensor_tensor(
            out=phi[:], in0=prod1[:], scalar=1.0 / (2.0 * math.pi), in1=prod3[:, 2:3], op0=ALU.mult, op1=ALU.mult
        )

        par_i = const.tile([P, 1], I32, name="par_i")
        nc.vector.tensor_single_scalar(out=par_i[:], in_=pidx_i[:], scalar=1, op=ALU.bitwise_and)
        par_f = const.tile([P, 1], F32, name="par_f")
        nc.vector.tensor_copy(out=par_f[:], in_=par_i[:])
        quarter = const.tile([P, 2], F32, name="quarter")
        nc.vector.tensor_scalar(out=quarter[:, 0:1], in0=par_f[:], scalar1=-0.25, scalar2=0.25, op0=ALU.mult, op1=ALU.add)
        nc.vector.tensor_scalar(out=quarter[:, 1:2], in0=par_f[:], scalar1=0.25, scalar2=None, op0=ALU.mult)
        sgn = const.tile([P, 1], F32, name="sgn")
        nc.vector.tensor_scalar(out=sgn[:], in0=par_f[:], scalar1=-2.0, scalar2=1.0, op0=ALU.mult, op1=ALU.add)
        hcol_f = const.tile([P, HEADS], F32, name="hcol_f")
        nc.vector.tensor_copy(out=hcol_f[:], in_=hcol_i[:])

        turns = const.tile([P, 2 * HEADS], F32, name="turns")
        turns_v = turns[:].rearrange("p (h e) -> p h e", e=2)
        for e in range(2):
            nc.vector.tensor_scalar(
                out=turns_v[:, :, e], in0=hcol_f[:], scalar1=phi[:, 0:1], scalar2=quarter[:, e : e + 1],
                op0=ALU.mult, op1=ALU.add,
            )
        red1 = const.tile([P, 2 * HEADS], F32, name="red1")
        nc.vector.scalar_tensor_tensor(out=red1[:], in0=turns[:], scalar=0.5, in1=turns[:], op0=ALU.is_gt, op1=ALU.subtract)
        red2 = const.tile([P, 2 * HEADS], F32, name="red2")
        nc.vector.scalar_tensor_tensor(out=red2[:], in0=turns[:], scalar=1.5, in1=red1[:], op0=ALU.is_gt, op1=ALU.add)
        red3 = const.tile([P, 2 * HEADS], F32, name="red3")
        nc.vector.scalar_tensor_tensor(out=red3[:], in0=turns[:], scalar=2.5, in1=red2[:], op0=ALU.is_gt, op1=ALU.add)
        trig = const.tile([P, 2 * HEADS], F32, name="trig")
        nc.scalar.activation(out=trig[:], in_=red3[:], func=ACT.Sin, scale=-2.0 * math.pi)
        trig_v = trig[:].rearrange("p (h e) -> p h e", e=2)
        val = const.tile([P, 2 * HEADS], F32, name="val")
        val_v = val[:].rearrange("p (h e) -> p h e", e=2)
        nc.vector.tensor_scalar(out=val_v[:, :, 0], in0=trig_v[:, :, 0], scalar1=sgn[:, 0:1], scalar2=None, op0=ALU.mult)
        nc.vector.tensor_copy(out=val_v[:, :, 1], in_=trig_v[:, :, 1])

        ident_v = ident[:].rearrange("p (i e) -> p i e", e=2)
        pair = const.tile([P, HEAD // 2], F32, name="pair")
        nc.vector.tensor_tensor(out=pair[:], in0=ident_v[:, :, 0], in1=ident_v[:, :, 1], op=ALU.add)
        rot = const.tile([P, HEADS * HEAD], F32, name="rot")
        rot_shape = [P, HEADS, HEAD // 2, 2]
        nc.vector.tensor_tensor(
            out=rot[:].rearrange("p (h i e) -> p h i e", h=HEADS, e=2),
            in0=pair[:].unsqueeze(1).unsqueeze(3).to_broadcast(rot_shape),
            in1=val_v.unsqueeze(2).to_broadcast(rot_shape),
            op=ALU.mult,
        )

        gx = const.tile([P, TOKENS * N_PASS * PACK], BF16, name="gx", align_bytes=64)
        gx_v = gx[:].bitcast(F32).rearrange("p (c b t u) -> p c b t u", c=N_PASS, b=N_BATCH, t=P, u=2)
        xc = const.tile([P, N_PASS * TOKENS], U32, name="xc", align_bytes=64)
        xs = const.tile([P, N_PASS * TOKENS], U8, name="xs", align_bytes=64)
        for b in range(N_BATCH):
            xw = x_sb[b][:].bitcast(F32).rearrange("t (c p u) -> t c u p", c=N_PASS, p=P, u=2)
            for ch in range(2):
                xt = bank(2 * b + ch, [P, 2, 2, P], "xt")
                for cc in range(2):
                    for u in range(2):
                        nc.tensor.transpose(xt[:, cc, u, :], xw[:, 2 * ch + cc, u, :], ident[:])
                nc.scalar.copy(
                    out=gx_v[:, 2 * ch : 2 * ch + 2, b, :, :], in_=xt[:].rearrange("p c u t -> p c t u")
                )
        out_rows = [[outs[m][b].rearrange("s h d -> s (h d)") for b in range(N_BATCH)] for m in range(3)]

        def chunks_of(n):
            t, c0, width = UNITS[n]
            return range(c0 // CHUNK, (c0 + width) // CHUNK)

        def last_unit(m, j):
            return max(n for n in range(N_UNITS) if UNITS[n][0] == m * N_PASS + N_PASS - 1 and j in chunks_of(n))

        def on_vector(j, b):
            return j >= N_CHUNK - 2 and b == N_BATCH - 1

        plan = {}
        for m in range(2):
            r_te = -ROT_EVERY
            for j in range(N_CHUNK):
                r_te = max(last_unit(m, j) + TE_AFTER, r_te + ROT_EVERY)
                plan[r_te] = plan.get(r_te, []) + [("te", m, j)]
                plan[r_te + OE_AFTER] = plan.get(r_te + OE_AFTER, []) + [("oe", m, j)]
        for j in range(N_CHUNK):
            r_ve = last_unit(2, j) + 1 + (1 if j == 1 else 0)
            plan[r_ve] = plan.get(r_ve, []) + [("ve", 2, j)]
        n_rounds = max(plan) + 1

        def v_cols_of(n):
            banks_out = sum(
                sum(1 for b in range(N_BATCH) if kind != "ve" or not on_vector(j, b))
                for kind, m, j in plan.get(n - LEAD, [])
            )
            width = UNITS[n][2]
            return min(width, V_COLS_BASE * width // CHUNK + V_COLS_STEP * banks_out)

        raws = {}
        groupeds = {}
        codes = {}
        scales = {}
        acc = {}
        tsb = {}
        rotated = {}
        osb = {}

        def load(t):
            raws[t] = rawp.tile([P, PACK, DM], BF16, name="raw", tag="raw")
            m, c = divmod(t, N_PASS)
            nc.sync.dma_start(
                out=raws[t][:],
                in_=weights[m][c * K_PASS : (c + 1) * K_PASS, :].rearrange("(p j) w -> p j w", j=PACK),
            )

        def load_next(n):
            t, c0, width = UNITS[n]
            if c0 + width == DM and t + RAW_BUFS < N_SLABS:
                load(t + RAW_BUFS)

        def regroup(copy, n, lo, hi):
            if lo == hi:
                return
            t, c0, width = UNITS[n]
            copy(
                out=groupeds[n][:, lo * PACK : hi * PACK].rearrange("p (c i u v) -> p c u i v", i=RUN, u=2, v=2),
                in_=raws[t][:, :, c0 + lo : c0 + hi].rearrange("p (u v) (c i) -> p c u i v", u=2, i=RUN),
            )

        def scalar_cut(n):
            lo, hi = v_cols_of(n), UNITS[n][2]
            if not any(kind == "oe" for kind, m, j in plan.get(n - LEAD, [])):
                return hi
            return lo + (hi - lo) // 16 * 8

        def new_grouped(n):
            groupeds[n] = grpp.tile([P, UNITS[n][2] * PACK], BF16, name="grouped", tag="grouped", align_bytes=64)

        def quantise(n):
            width = UNITS[n][2]
            codes[n] = codep.tile([P, width], U32, name="codes", tag="codes", align_bytes=64)
            scales[n] = codep.tile([P, width], U8, name="scales", tag="scales", align_bytes=64)
            nc.vector.quantize_mx(out=codes[n][:].bitcast(FP8X4), scales=scales[n][:], in_=groupeds[n][:])

        def multiply(n, j):
            t, c0, width = UNITS[n]
            m, c = divmod(t, N_PASS)
            at = j * CHUNK - c0
            for i in range(2):
                if c == 0:
                    acc[(i, j)] = bank(2 * j + i, [P, CHUNK], "acc")
                if m < 2:
                    for e in range(2):
                        w_cols = slice(at + (2 * i + e) * HEAD, at + (2 * i + e + 1) * HEAD)
                        nc.tensor.matmul_mx(
                            out=acc[(i, j)][:, e * TOKENS : (e + 1) * TOKENS],
                            lhsT=codes[n][:, w_cols].bitcast(FP8X4),
                            lhsT_scale=scales[n][:, w_cols],
                            rhs=xc[:, c * TOKENS : (c + 1) * TOKENS].bitcast(FP8X4),
                            rhs_scale=xs[:, c * TOKENS : (c + 1) * TOKENS],
                            start=(c == 0 and e == 0),
                            stop=(c == N_PASS - 1 and e == 1),
                        )
                else:
                    x_b = slice(c * TOKENS + i * P, c * TOKENS + (i + 1) * P)
                    nc.tensor.matmul_mx(
                        out=acc[(i, j)][:],
                        lhsT=xc[:, x_b].bitcast(FP8X4),
                        lhsT_scale=xs[:, x_b],
                        rhs=codes[n][:, at : at + CHUNK].bitcast(FP8X4),
                        rhs_scale=scales[n][:, at : at + CHUNK],
                        start=(c == 0),
                        stop=(c == N_PASS - 1),
                    )

        def sums_out_and_rotate(j):
            for i in range(2):
                tsb[i] = tsbp.tile([P, CHUNK], F32, name="tsb", tag="tsb")
                nc.scalar.copy(out=tsb[i][:], in_=acc[(i, j)][:])
            for b in range(N_BATCH):
                rotated[(b, j)] = bank(2 * j + b, [P, CHUNK], "rotated")
                for hh in range(4):
                    lo = (hh % 2) * TOKENS + b * P
                    h = 4 * j + hh
                    nc.tensor.matmul(
                        out=rotated[(b, j)][:, hh * HEAD : (hh + 1) * HEAD],
                        lhsT=tsb[hh // 2][:, lo : lo + P],
                        rhs=rot[:, h * HEAD : (h + 1) * HEAD],
                        start=True,
                        stop=True,
                    )

        def rotated_out(m, j):
            for b in range(N_BATCH):
                if j % 2 == 0:
                    osb[b] = outp.tile([P, 2 * CHUNK], F32, name="osb", tag="osb")
                nc.scalar.copy(out=osb[b][:, (j % 2) * CHUNK : (j % 2 + 1) * CHUNK], in_=rotated[(b, j)][:])
                if j % 2 == 1:
                    nc.sync.dma_start(out=out_rows[m][b][:, (j - 1) * CHUNK : (j + 1) * CHUNK], in_=osb[b][:])

        def v_out(j, by_vector):
            for b in range(N_BATCH):
                if on_vector(j, b) != by_vector:
                    continue
                vsb = vout.tile([P, CHUNK], F32, name="vsb", tag="vsb")
                if by_vector:
                    nc.vector.tensor_copy(out=vsb[:], in_=acc[(b, j)][:])
                else:
                    nc.scalar.copy(out=vsb[:], in_=acc[(b, j)][:])
                nc.sync.dma_start(out=out_rows[2][b][:, j * CHUNK : (j + 1) * CHUNK], in_=vsb[:])

        for t in range(RAW_BUFS):
            load(t)
        for ch in range(2):
            nc.vector.quantize_mx(
                out=xc[:, ch * 512 : (ch + 1) * 512].bitcast(FP8X4),
                scales=xs[:, ch * 512 : (ch + 1) * 512],
                in_=gx[:, ch * 2048 : (ch + 1) * 2048],
            )
        for n in range(LEAD):
            new_grouped(n)
            regroup(nc.vector.tensor_copy, n, 0, v_cols_of(n))
            regroup(nc.scalar.copy, n, v_cols_of(n), UNITS[n][2])
            load_next(n)

        waiting = []
        held = [False] * N_CHUNK
        for r in range(n_rounds):
            ahead = r + LEAD
            for kind, m, j in plan.get(r, []):
                if kind == "te":
                    sums_out_and_rotate(j)
                elif kind == "ve":
                    v_out(j, False)
            if ahead < N_UNITS:
                new_grouped(ahead)
                regroup(nc.scalar.copy, ahead, v_cols_of(ahead), scalar_cut(ahead))
            for kind, m, j in plan.get(r, []):
                if kind == "oe":
                    rotated_out(m, j)
                    held[j] = False
            if ahead < N_UNITS:
                regroup(nc.scalar.copy, ahead, scalar_cut(ahead), UNITS[ahead][2])
            if r < N_UNITS:
                quantise(r)
                waiting.extend((r, j) for j in chunks_of(r))
            if ahead < N_UNITS:
                regroup(nc.vector.tensor_copy, ahead, 0, v_cols_of(ahead))
                load_next(ahead)
            for kind, m, j in plan.get(r, []):
                if kind == "ve":
                    v_out(j, True)
            still = []
            for n, j in waiting:
                m, c = divmod(UNITS[n][0], N_PASS)
                if (c == 0 and held[j]) or any(w[1] == j for w in still):
                    still.append((n, j))
                else:
                    multiply(n, j)
                    if c == N_PASS - 1 and m < 2:
                        held[j] = True
            waiting = still
        assert not waiting
